import numpy as np
import ml_dtypes


def mxq(x, axis, fmt="e4m3"):
    dtype, down = {"e4m3": (ml_dtypes.float8_e4m3fn, 7), "e5m2": (ml_dtypes.float8_e5m2, 14)}[fmt]
    v = np.moveaxis(np.asarray(x, np.float32).astype(ml_dtypes.bfloat16).astype(np.float64), axis, -1)
    blocks = v.reshape(v.shape[:-1] + (-1, 32))
    amax = np.abs(blocks).max(-1, keepdims=True)
    byte = np.maximum(np.where(amax > 0, np.frexp(amax)[1] - 1 + 127, 0) - down, 1)
    scale = np.exp2(byte - 127.0)
    codes = (blocks / scale).astype(np.float32).astype(dtype).astype(np.float64)
    return np.moveaxis((codes * scale).reshape(v.shape), -1, axis)


WIDE = False


def mx_kscale(k):
    if not WIDE:
        return np.ones(k)
    levels = np.array([30, -30])
    if k % 512:
        return np.exp2(np.random.permutation(np.resize(levels, k // 32))).repeat(32)
    a = np.empty((k // 512, 16))
    for p in range(k // 512):
        a[p, :8] = np.random.permutation(np.resize(levels, 8))
        for g in range(8):
            far = levels[np.abs(levels - a[p, g]) >= 10]
            a[p, g + 8] = far[np.random.randint(len(far))]
    return np.exp2(a.ravel()).repeat(32)


BF16 = ml_dtypes.bfloat16


def bf(x):
    return np.asarray(x, np.float32).astype(BF16)


def f64(x):
    return np.asarray(x).astype(np.float64)


E2M1 = np.array([0.0, 0.5, 1.0, 1.5, 2.0, 3.0, 4.0, 6.0, -0.0, -0.5, -1.0, -1.5, -2.0, -3.0, -4.0, -6.0])


def pack_weight(w, fmt):
    k, n = w.shape
    w = f64(bf(w)).reshape(k // 32, 32, n)
    amax = np.abs(w).max(1)
    if fmt == "e4m3":
        byte = np.frexp(amax)[1] - 1 + 127 - 7
    else:
        mant, ex = np.frexp(amax / 6.0)
        byte = np.where(mant > 0.5, ex, ex - 1) + 127
    byte = np.clip(np.where(amax > 0, byte, 1), 1, 254)
    scaled = (w * np.exp2(127.0 - byte)[:, None, :]).reshape(k, n).astype(np.float32)
    by_word = np.ascontiguousarray(scaled.reshape(k // 512, 128, 4, n).transpose(0, 1, 3, 2))
    if fmt == "e4m3":
        words = by_word.astype(ml_dtypes.float8_e4m3fn).view(np.uint8)
    else:
        c = by_word.astype(ml_dtypes.float4_e2m1fn).view(np.uint8) & 0xF
        words = c[..., 0::2] | (c[..., 1::2] << 4)
    return np.ascontiguousarray(words), np.ascontiguousarray(byte.astype(np.uint8).reshape(k // 512, 16, n))


def unpack_weight(words, scales, fmt):
    g, p, n, _ = words.shape
    if fmt == "e4m3":
        vals = np.ascontiguousarray(words).view(ml_dtypes.float8_e4m3fn).astype(np.float64)
    else:
        nib = np.empty((g, p, n, 4), np.uint8)
        nib[..., 0::2] = words & 0xF
        nib[..., 1::2] = words >> 4
        vals = E2M1[nib]
    vals = vals * np.repeat(np.exp2(scales.astype(np.float64) - 127.0), 8, axis=1)[..., None]
    return vals.transpose(0, 1, 3, 2).reshape(g * 512, n)

def pack4(w):
    words, scales = pack_weight(w, "e2m1")
    return words.reshape(words.shape[0], 128, -1), scales


def unpack4(words, scales):
    return unpack_weight(words.reshape(words.shape[0], 128, -1, 2), scales, "e2m1")


B, L, C, H, BLK = 2, 512, 1024, 16, 128
D = C // H
MAX_SCALE_MUL = np.log(100.0)
EPS = 1e-12


def l2norm(t):
    n = np.sqrt(np.sum(t * t, axis=-1, keepdims=True))
    return t / np.maximum(n, EPS)


def setup_inputs():
    s = mx_kscale(C)
    lsm = np.linspace(np.log(4.0), MAX_SCALE_MUL + 1.0, H) + 0.05 * np.random.standard_normal(H)
    x = bf(np.random.standard_normal((B, L, C)) * s)
    w = np.random.standard_normal((3 * C, C)) / np.sqrt(C) / s[None, :]
    words, scales = pack4(np.ascontiguousarray(w.T))
    q_bias = bf(np.random.standard_normal(C) * 0.3)
    v_bias = bf(np.random.standard_normal(C) * 0.3)
    return {"x": x,
            "W_qkv_words": words,
            "W_qkv_scales": scales,
            "q_bias": q_bias,
            "v_bias": v_bias,
            "log_scale_mul": bf(lsm.reshape(1, H, 1, 1))}


def reference(x, W_qkv_words, W_qkv_scales, q_bias, v_bias, log_scale_mul):
    qb = f64(q_bias)
    bias = np.concatenate([qb, np.zeros_like(qb), f64(v_bias)])
    qkv = (mxq(f64(x), 2, "e5m2") @ unpack4(W_qkv_words, W_qkv_scales)) + bias
    qkv = qkv.reshape(B, L, 3, H, D)
    q, k, v = np.moveaxis(qkv, 2, 0)
    q = np.swapaxes(q, 1, 2)
    k = np.swapaxes(k, 1, 2)
    v = np.swapaxes(v, 1, 2)
    scale_mul = np.exp(np.minimum(f64(log_scale_mul), MAX_SCALE_MUL))
    q = l2norm(q) * scale_mul
    k = l2norm(k)
    return q, k, v

@@ -1,0 +1,321 @@
+import math
+from contextlib import ExitStack
+
+import concourse.mybir as mybir
+from concourse.masks import make_identity
+
+B, L, C, H = 2, 512, 1024, 16
+D = C // H
+FLOPS = 2 * B * L * C * 3 * C
+
+F32 = mybir.dt.float32
+BF16 = mybir.dt.bfloat16
+I32 = mybir.dt.int32
+U32 = mybir.dt.uint32
+U8 = mybir.dt.uint8
+E5M2X4 = mybir.dt.float8_e5m2_x4
+E2M1X4 = mybir.dt.float4_e2m1fn_x4
+ALU = mybir.AluOpType
+ACT = mybir.ActivationFunctionType
+
+P = 128
+PASSES = C // 512
+N = 512
+HEADS = N // D
+J = L // P
+MAX_LOG_SCALE = math.log(100.0)
+MAX_INV_NORM = 1e12
+K_LAG = 3
+
+
+def tile_selfattention_pa_kernel(
+    tc, x, W_qkv_words, W_qkv_scales, q_bias, v_bias, log_scale_mul, out_0, out_1, out_2
+):
+    nc = tc.nc
+    outs = {"q": out_0, "k": out_1, "v": out_2}
+    first_chunk = {"q": 0, "k": 2, "v": 4}
+
+    groups = []
+    for b in range(B):
+        for c in range(2):
+            last = b == B - 1 and c == 1
+            for kind in ("q", "k", "v") if last else ("k", "q", "v"):
+                groups.append((kind, b, c))
+    n_banks = len(groups) * J
+
+    with ExitStack() as ctx:
+        keep = ctx.enter_context(tc.tile_pool(name="keep", bufs=1))
+        work = ctx.enter_context(tc.tile_pool(name="work", bufs=3))
+        psum = ctx.enter_context(tc.psum_pool(name="psum", bufs=8))
+        ctx.enter_context(tc.manual_schedule())
+
+        ident = keep.tile([P, P], F32, name="ident")
+        make_identity(nc, ident[:])
+        rows = keep.tile([P, 2 * C], BF16, name="rows")
+        nc.vector.memset(rows[:].bitcast(I32), 0)
+        ones = keep.tile([P, P], BF16, name="ones")
+        nc.vector.memset(ones[:], 1.0)
+        plane = keep.tile([P, PASSES, 3 * C], U8, name="plane", align_bytes=64)
+        nc.vector.memset(plane[:].bitcast(I32), 0)
+
+        log_scale = keep.tile([P, H], BF16, name="log_scale")
+        nc.scalar.dma_start(
+            out=log_scale[:], in_=log_scale_mul.rearrange("a h b c -> (a h b c)").partition_broadcast(P)
+        )
+        nc.scalar.dma_start(out=rows[0:1, 0:C], in_=q_bias.rearrange("(o n) -> o n", o=1))
+        nc.scalar.dma_start(out=rows[0:1, C : 2 * C], in_=v_bias.rearrange("(o n) -> o n", o=1))
+
+        x_raw = {}
+        w_codes = {}
+
+        def load_x(b, j):
+            t = keep.tile([P, C], BF16, name="x_%d_%d" % (b, j))
+            nc.sync.dma_start(out=t[:], in_=x[b].rearrange("(p j) c -> p j c", j=J)[:, j, :])
+            x_raw[(b, j)] = t
+
+        def load_w(chunk):
+            t = keep.tile([P, PASSES, 2 * N], U8, name="w_%d" % chunk, align_bytes=64)
+            src = W_qkv_words[:, :, 2 * N * chunk : 2 * N * (chunk + 1)].rearrange("g p w -> p g w")
+            nc.sync.dma_start(out=t[:].bitcast(I32), in_=src.bitcast(I32))
+            w_codes[chunk] = t
+
+        chunks = [first_chunk[kind] + c for kind, b, c in groups if b == 0]
+        load_x(0, 0)
+        load_x(0, 1)
+        load_w(chunks[0])
+        for q in range(4):
+            nc.sync.dma_start(
+                out=plane[32 * q : 32 * q + 4, :, :].bitcast(I32),
+                in_=W_qkv_scales[:, 4 * q : 4 * q + 4, :].rearrange("g r n -> r g n").bitcast(I32),
+            )
+        load_x(0, 2)
+        load_x(0, 3)
+        for j in range(J):
+            load_x(1, j)
+        for chunk in chunks[1:]:
+            load_w(chunk)
+
+        clamped = keep.tile([P, H], F32, name="clamped")
+        nc.vector.tensor_scalar(clamped[:], log_scale[:], MAX_LOG_SCALE, None, op0=ALU.min)
+        scale = keep.tile([P, H], F32, name="scale")
+        nc.scalar.activation(scale[:], clamped[:], ACT.Exp)
+
+        bias = {}
+        bias_banks = {}
+        for i, kind in enumerate(("q", "v")):
+            bank = psum.tile([P, C], BF16, name="bias_bank_%s" % kind, tag="bank")
+            for half in range(2):
+                nc.tensor.matmul(
+                    bank[:, N * half : N * (half + 1)],
+                    lhsT=ones[:],
+                    rhs=rows[:, C * i + N * half : C * i + N * (half + 1)],
+                    start=True,
+                    stop=True,
+                )
+            bias_banks[kind] = bank
+        for kind in ("q", "v"):
+            t = keep.tile([P, C], BF16, name="bias_%s" % kind)
+            nc.vector.tensor_copy(out=t[:], in_=bias_banks[kind][:])
+            bias[kind] = t
+
+        pending = []
+
+        def flush():
+            ready = list(pending)
+            pending.clear()
+            for emit in ready:
+                emit()
+
+        x_banks = {}
+        x_grouped = {}
+        x_codes = {}
+        x_scales = {}
+
+        def transpose_x(b, j):
+            words = x_raw[(b, j)][:].bitcast(F32)
+            bank = psum.tile([P, N], F32, name="xt_%d_%d" % (b, j), tag="bank")
+            for g in range(PASSES):
+                for u in range(2):
+                    col = P * (2 * g + u)
+                    nc.tensor.transpose(bank[:, col : col + P], words[:, 256 * g + u : 256 * (g + 1) : 2], ident[:])
+            x_banks[(b, j)] = bank
+
+        def copy_x(b, j, on_vector):
+            t = keep.tile([P, C], BF16, name="xg_%d_%d" % (b, j), align_bytes=64)
+            dst = t[:].bitcast(F32).rearrange("p (g r u) -> p g r u", g=PASSES, u=2)
+            src = x_banks[(b, j)][:].rearrange("p (g u r) -> p g r u", g=PASSES, u=2)
+            if on_vector:
+                nc.vector.tensor_copy(out=dst, in_=src)
+            else:
+                nc.scalar.copy(out=dst, in_=src)
+            x_grouped[(b, j)] = t
+
+        def quantize_x(b, j):
+            codes = keep.tile([P, PASSES * P], U32, name="xc_%d_%d" % (b, j), align_bytes=64)
+            scales = keep.tile([P, PASSES * P], U8, name="xs_%d_%d" % (b, j), align_bytes=64)
+            nc.vector.quantize_mx(out=codes[:].bitcast(E5M2X4), scales=scales[:], in_=x_grouped[(b, j)][:])
+            x_codes[(b, j)] = codes
+            x_scales[(b, j)] = scales
+
+        for j in range(J):
+            transpose_x(0, j)
+            copy_x(0, j, False)
+            quantize_x(0, j)
+
+        banks = {}
+        stage = {}
+        q_raw = {}
+        sums = {}
+        inv_norm = {}
+        for kind, b, c in groups:
+            stage[(kind, b, c)] = keep.tile([P, HEADS, J, D], F32, name="stage_%s_%d_%d" % (kind, b, c))
+
+        def matmul(n):
+            kind, b, c = groups[n // J]
+            j = n % J
+            chunk = first_chunk[kind] + c
+            bank = psum.tile([P, N], F32, name="acc_%d" % n, tag="bank")
+            for g in range(PASSES):
+                nc.tensor.matmul_mx(
+                    out=bank[:],
+                    lhsT=x_codes[(b, j)][:, P * g : P * (g + 1)].bitcast(E5M2X4),
+                    lhsT_scale=x_scales[(b, j)][:, P * g : P * (g + 1)],
+                    rhs=w_codes[chunk][:, g, :].bitcast(E2M1X4),
+                    rhs_scale=plane[:, g, N * chunk : N * (chunk + 1)],
+                    start=(g == 0),
+                    stop=(g == PASSES - 1),
+                )
+            banks[n] = bank
+
+        stored = []
+
+        def store(group):
+            kind, b, c = group
+            stored.append(group)
+            dst = outs[kind][b, HEADS * c : HEADS * (c + 1), :, :].rearrange("h (p j) d -> p h (j d)", j=J)
+            nc.sync.dma_start(out=dst, in_=stage[group][:].rearrange("p h j d -> p h (j d)"))
+
+        def add_bias(n):
+            group = groups[n // J]
+            kind, b, c = group
+            j = n % J
+            bias_cols = bias[kind][:, N * c : N * (c + 1)]
+            if kind == "v":
+                nc.vector.tensor_tensor(
+                    stage[group][:, :, j, :],
+                    banks[n][:].rearrange("p (h d) -> p h d", d=D),
+                    bias_cols.rearrange("p (h d) -> p h d", d=D),
+                    op=ALU.add,
+                )
+                if j == J - 1:
+                    store(group)
+            else:
+                if j % 2 == 0:
+                    q_raw[n // 2] = work.tile([P, 2, N], F32, name="q_raw_%d" % n, tag="q_raw", bufs=4)
+                nc.vector.tensor_tensor(q_raw[n // 2][:, j % 2, :], banks[n][:], bias_cols, op=ALU.add)
+
+        def squares(src, dst):
+            junk = work.tile([P, N], F32, name="junk", tag="junk", bufs=3)
+            for h in range(HEADS):
+                nc.scalar.activation(
+                    junk[:, D * h : D * (h + 1)], src[:, D * h : D * (h + 1)], ACT.Square, accum_out=dst[:, h : h + 1]
+                )
+                if h == 1:
+                    flush()
+
+        def k_squares(n):
+            total = keep.tile([P, HEADS], F32, name="k_sum_%d" % n)
+            squares(banks[n][:], total[:])
+
+            def root():
+                r = keep.tile([P, HEADS], F32, name="k_inv_%d" % n)
+                nc.scalar.activation(r[:], total[:], ACT.Abs_reciprocal_sqrt)
+                inv_norm[n] = r
+
+            pending.append(root)
+
+        def k_normalise(n):
+            group = groups[n // J]
+            j = n % J
+            if n not in inv_norm:
+                flush()
+            nc.vector.scalar_tensor_tensor(
+                out=stage[group][:, :, j, :],
+                in0=inv_norm[n][:].unsqueeze(2).to_broadcast([P, HEADS, D]),
+                scalar=MAX_INV_NORM,
+                in1=banks[n][:].rearrange("p (h d) -> p h d", d=D),
+                op0=ALU.min,
+                op1=ALU.mult,
+            )
+            if j == J - 1:
+                store(group)
+
+        q_done = []
+
+        def q_squares(n):
+            group = groups[n // J]
+            kind, b, c = group
+            j = n % J
+            pair = n // 2
+            if j % 2 == 0:
+                sums[pair] = keep.tile([P, 2, HEADS], F32, name="q_sum_%d" % n)
+            squares(q_raw[pair][:, j % 2, :], sums[pair][:, j % 2, :])
+            if j % 2 == 0:
+                return
+
+            def normalise():
+                r = keep.tile([P, 2, HEADS], F32, name="q_inv_%d" % n)
+                nc.scalar.activation(r[:], sums[pair][:], ACT.Abs_reciprocal_sqrt)
+                capped = keep.tile([P, 2, HEADS], F32, name="q_cap_%d" % n)
+                nc.gpsimd.tensor_scalar(capped[:], r[:], MAX_INV_NORM, 0.0, op0=ALU.min, op1=ALU.max)
+                factor = keep.tile([P, 2, HEADS], F32, name="q_fac_%d" % n)
+                nc.gpsimd.tensor_tensor(
+                    factor[:],
+                    capped[:],
+                    scale[:, HEADS * c : HEADS * (c + 1)].unsqueeze(1).to_broadcast([P, 2, HEADS]),
+                    op=ALU.mult,
+                )
+                nc.gpsimd.tensor_tensor(
+                    stage[group][:, :, j - 1 : j + 1, :].rearrange("p h j d -> p j h d"),
+                    q_raw[pair][:].rearrange("p j (h d) -> p j h d", d=D),
+                    factor[:].unsqueeze(3).to_broadcast([P, 2, HEADS, D]),
+                    op=ALU.mult,
+                )
+                if j == J - 1:
+                    q_done.append(group)
+
+            pending.append(normalise)
+
+        def kind_of(n):
+            return groups[n // J][0] if 0 <= n < n_banks else None
+
+        for n in range(n_banks + K_LAG + 1):
+            if n == J:
+                for j in range(J):
+                    transpose_x(1, j)
+                k_squares(n - 1)
+                k_normalise(n - K_LAG)
+                for j in range(J):
+                    copy_x(1, j, j % 2 == 0)
+                    if j == 1:
+                        flush()
+                        k_normalise(n - K_LAG + 1)
+                    if j > 0:
+                        quantize_x(1, j - 1)
+                k_normalise(n - K_LAG + 2)
+                quantize_x(1, J - 1)
+            if n < n_banks:
+                matmul(n)
+            if kind_of(n - 2) == "q":
+                q_squares(n - 2)
+            if kind_of(n - 1) == "k" and n != J:
+                k_squares(n - 1)
+            if kind_of(n - 1) in ("q", "v"):
+                add_bias(n - 1)
+            if kind_of(n - K_LAG) == "k" and not (J <= n < J + K_LAG):
+                k_normalise(n - K_LAG)
+            for group in list(q_done):
+                if ("v",) + group[1:] in stored or group == groups[-3]:
+                    store(group)
+                    q_done.remove(group)
+        assert len(stored) == len(groups) and not pending

@@ -19,13 +19,34 @@ ALU = mybir.AluOpType
 ACT = mybir.ActivationFunctionType
 
 P = 128
-PASSES = C // 512
-N = 512
-HEADS = N // D
-J = L // P
+K_PASS = 4 * P
+PASSES = C // K_PASS
+TILES = L // P
+BANK = 512
+CHUNK = 512
+UNIT_HEADS = 4
+UNIT_COLS = UNIT_HEADS * D
+UNITS = B * H // UNIT_HEADS
+BANK_TILES = BANK // UNIT_COLS
+BANK_SUMS = BANK_TILES * UNIT_HEADS
+FIRST_COL = {"q": 0, "k": C, "v": 2 * C}
+DMA_ALIGN = 256
+MX_ALIGN = 64
 MAX_LOG_SCALE = math.log(100.0)
-MAX_INV_NORM = 1e12
-K_LAG = 3
+EPS = 1e-12
+LEAD_PAIRS = 3
+EARLY_CHUNKS = 3
+
+
+def unit_order():
+    order = []
+    for u in range(LEAD_PAIRS):
+        order.extend([("k", u), ("v", u)])
+    others = [(kind, u) for u in range(LEAD_PAIRS, UNITS) for kind in ("v", "k")]
+    for u in range(UNITS):
+        order.extend([("q", u), others[u]])
+    order.extend(others[UNITS:])
+    return order
 
 
 def tile_selfattention_pa_kernel(
@@ -33,289 +54,219 @@ def tile_selfattention_pa_kernel(
 ):
     nc = tc.nc
     outs = {"q": out_0, "k": out_1, "v": out_2}
-    first_chunk = {"q": 0, "k": 2, "v": 4}
-
-    groups = []
-    for b in range(B):
-        for c in range(2):
-            last = b == B - 1 and c == 1
-            for kind in ("q", "k", "v") if last else ("k", "q", "v"):
-                groups.append((kind, b, c))
-    n_banks = len(groups) * J
+    per_batch = UNITS // B
+    units = [(kind, u // per_batch, UNIT_HEADS * (u % per_batch)) for kind, u in unit_order()]
 
     with ExitStack() as ctx:
         keep = ctx.enter_context(tc.tile_pool(name="keep", bufs=1))
-        work = ctx.enter_context(tc.tile_pool(name="work", bufs=3))
+        work = ctx.enter_context(tc.tile_pool(name="work", bufs=4))
         psum = ctx.enter_context(tc.psum_pool(name="psum", bufs=8))
-        ctx.enter_context(tc.manual_schedule())
+        ctx.enter_context(tc.manual_schedule(engines={mybir.EngineType.PE}))
 
-        ident = keep.tile([P, P], F32, name="ident")
-        make_identity(nc, ident[:])
-        rows = keep.tile([P, 2 * C], BF16, name="rows")
-        nc.vector.memset(rows[:].bitcast(I32), 0)
+        identity = keep.tile([P, P], F32, name="identity")
+        make_identity(nc, identity[:])
+        bias_rows = keep.tile([P, 2 * C], BF16, name="bias_rows")
+        nc.vector.memset(bias_rows[:].bitcast(I32), 0)
+        w_scales = keep.tile([P, PASSES, 3 * C], U8, name="w_scales", align_bytes=DMA_ALIGN)
+        nc.vector.memset(w_scales[:].bitcast(I32), 0)
         ones = keep.tile([P, P], BF16, name="ones")
-        nc.vector.memset(ones[:], 1.0)
-        plane = keep.tile([P, PASSES, 3 * C], U8, name="plane", align_bytes=64)
-        nc.vector.memset(plane[:].bitcast(I32), 0)
+        nc.gpsimd.memset(ones[:], 1.0)
 
         log_scale = keep.tile([P, H], BF16, name="log_scale")
         nc.scalar.dma_start(
             out=log_scale[:], in_=log_scale_mul.rearrange("a h b c -> (a h b c)").partition_broadcast(P)
         )
-        nc.scalar.dma_start(out=rows[0:1, 0:C], in_=q_bias.rearrange("(o n) -> o n", o=1))
-        nc.scalar.dma_start(out=rows[0:1, C : 2 * C], in_=v_bias.rearrange("(o n) -> o n", o=1))
+        nc.scalar.dma_start(out=bias_rows[0:1, 0:C], in_=q_bias.rearrange("(o n) -> o n", o=1))
+        nc.scalar.dma_start(out=bias_rows[0:1, C : 2 * C], in_=v_bias.rearrange("(o n) -> o n", o=1))
 
-        x_raw = {}
-        w_codes = {}
+        x_rows = {}
+        w_words = {}
 
         def load_x(b, j):
-            t = keep.tile([P, C], BF16, name="x_%d_%d" % (b, j))
-            nc.sync.dma_start(out=t[:], in_=x[b].rearrange("(p j) c -> p j c", j=J)[:, j, :])
-            x_raw[(b, j)] = t
+            rows = keep.tile([P, C], BF16, name="x_%d_%d" % (b, j), align_bytes=DMA_ALIGN)
+            nc.sync.dma_start(out=rows[:], in_=x[b].rearrange("(p j) c -> p j c", j=TILES)[:, j, :])
+            x_rows[(b, j)] = rows
 
         def load_w(chunk):
-            t = keep.tile([P, PASSES, 2 * N], U8, name="w_%d" % chunk, align_bytes=64)
-            src = W_qkv_words[:, :, 2 * N * chunk : 2 * N * (chunk + 1)].rearrange("g p w -> p g w")
-            nc.sync.dma_start(out=t[:].bitcast(I32), in_=src.bitcast(I32))
-            w_codes[chunk] = t
+            words = keep.tile([P, PASSES, 2 * CHUNK], U8, name="w_%d" % chunk, align_bytes=DMA_ALIGN)
+            src = W_qkv_words[:, :, 2 * CHUNK * chunk : 2 * CHUNK * (chunk + 1)].rearrange("g p w -> p g w")
+            nc.sync.dma_start(out=words[:].bitcast(I32), in_=src.bitcast(I32))
+            w_words[chunk] = words
 
-        chunks = [first_chunk[kind] + c for kind, b, c in groups if b == 0]
-        load_x(0, 0)
-        load_x(0, 1)
-        load_w(chunks[0])
-        for q in range(4):
-            nc.sync.dma_start(
-                out=plane[32 * q : 32 * q + 4, :, :].bitcast(I32),
-                in_=W_qkv_scales[:, 4 * q : 4 * q + 4, :].rearrange("g r n -> r g n").bitcast(I32),
-            )
-        load_x(0, 2)
-        load_x(0, 3)
-        for j in range(J):
-            load_x(1, j)
-        for chunk in chunks[1:]:
-            load_w(chunk)
+        chunks = []
+        for kind, b, h0 in units:
+            chunk = (FIRST_COL[kind] + D * h0) // CHUNK
+            if chunk not in chunks:
+                chunks.append(chunk)
+        with tc.manual_schedule(engines={mybir.EngineType.SP}):
+            load_x(0, 0)
+            load_x(0, 1)
+            load_w(chunks[0])
+            for quad in range(4):
+                nc.sync.dma_start(
+                    out=w_scales[32 * quad : 32 * quad + 4, :, :].bitcast(I32),
+                    in_=W_qkv_scales[:, 4 * quad : 4 * quad + 4, :].rearrange("g r n -> r g n").bitcast(I32),
+                )
+            load_x(0, 2)
+            load_x(0, 3)
+            for chunk in chunks[1:EARLY_CHUNKS]:
+                load_w(chunk)
+            for j in range(TILES):
+                load_x(1, j)
+            for chunk in chunks[EARLY_CHUNKS:]:
+                load_w(chunk)
 
         clamped = keep.tile([P, H], F32, name="clamped")
         nc.vector.tensor_scalar(clamped[:], log_scale[:], MAX_LOG_SCALE, None, op0=ALU.min)
-        scale = keep.tile([P, H], F32, name="scale")
-        nc.scalar.activation(scale[:], clamped[:], ACT.Exp)
+        inverse_scale = keep.tile([P, H], F32, name="inverse_scale")
+        nc.scalar.activation(inverse_scale[:], clamped[:], ACT.Exp, scale=-1.0)
+        root_scale = keep.tile([P, H], F32, name="root_scale")
+        nc.scalar.activation(root_scale[:], inverse_scale[:], ACT.Abs_reciprocal_sqrt)
+        head_scale = keep.tile([P, H], F32, name="head_scale")
+        nc.gpsimd.tensor_tensor(head_scale[:], root_scale[:], root_scale[:], op=ALU.mult)
 
         bias = {}
-        bias_banks = {}
         for i, kind in enumerate(("q", "v")):
-            bank = psum.tile([P, C], BF16, name="bias_bank_%s" % kind, tag="bank")
-            for half in range(2):
+            spread = psum.tile([P, C], BF16, name="bias_bank", tag="bank")
+            for col in range(0, C, BANK):
                 nc.tensor.matmul(
-                    bank[:, N * half : N * (half + 1)],
+                    spread[:, col : col + BANK],
                     lhsT=ones[:],
-                    rhs=rows[:, C * i + N * half : C * i + N * (half + 1)],
+                    rhs=bias_rows[:, C * i + col : C * i + col + BANK],
                     start=True,
                     stop=True,
                 )
-            bias_banks[kind] = bank
-        for kind in ("q", "v"):
-            t = keep.tile([P, C], BF16, name="bias_%s" % kind)
-            nc.vector.tensor_copy(out=t[:], in_=bias_banks[kind][:])
-            bias[kind] = t
+            bias[kind] = keep.tile([P, C], BF16, name="bias_%s" % kind)
+            nc.vector.tensor_copy(out=bias[kind][:], in_=spread[:])
 
-        pending = []
-
-        def flush():
-            ready = list(pending)
-            pending.clear()
-            for emit in ready:
-                emit()
-
-        x_banks = {}
-        x_grouped = {}
-        x_codes = {}
+        x_words = {}
         x_scales = {}
 
-        def transpose_x(b, j):
-            words = x_raw[(b, j)][:].bitcast(F32)
-            bank = psum.tile([P, N], F32, name="xt_%d_%d" % (b, j), tag="bank")
-            for g in range(PASSES):
-                for u in range(2):
-                    col = P * (2 * g + u)
-                    nc.tensor.transpose(bank[:, col : col + P], words[:, 256 * g + u : 256 * (g + 1) : 2], ident[:])
-            x_banks[(b, j)] = bank
-
-        def copy_x(b, j, on_vector):
-            t = keep.tile([P, C], BF16, name="xg_%d_%d" % (b, j), align_bytes=64)
-            dst = t[:].bitcast(F32).rearrange("p (g r u) -> p g r u", g=PASSES, u=2)
-            src = x_banks[(b, j)][:].rearrange("p (g u r) -> p g r u", g=PASSES, u=2)
-            if on_vector:
-                nc.vector.tensor_copy(out=dst, in_=src)
-            else:
-                nc.scalar.copy(out=dst, in_=src)
-            x_grouped[(b, j)] = t
-
-        def quantize_x(b, j):
-            codes = keep.tile([P, PASSES * P], U32, name="xc_%d_%d" % (b, j), align_bytes=64)
-            scales = keep.tile([P, PASSES * P], U8, name="xs_%d_%d" % (b, j), align_bytes=64)
-            nc.vector.quantize_mx(out=codes[:].bitcast(E5M2X4), scales=scales[:], in_=x_grouped[(b, j)][:])
-            x_codes[(b, j)] = codes
-            x_scales[(b, j)] = scales
-
-        for j in range(J):
-            transpose_x(0, j)
-            copy_x(0, j, False)
-            quantize_x(0, j)
-
-        banks = {}
-        stage = {}
-        q_raw = {}
-        sums = {}
-        inv_norm = {}
-        for kind, b, c in groups:
-            stage[(kind, b, c)] = keep.tile([P, HEADS, J, D], F32, name="stage_%s_%d_%d" % (kind, b, c))
-
-        def matmul(n):
-            kind, b, c = groups[n // J]
-            j = n % J
-            chunk = first_chunk[kind] + c
-            bank = psum.tile([P, N], F32, name="acc_%d" % n, tag="bank")
-            for g in range(PASSES):
-                nc.tensor.matmul_mx(
-                    out=bank[:],
-                    lhsT=x_codes[(b, j)][:, P * g : P * (g + 1)].bitcast(E5M2X4),
-                    lhsT_scale=x_scales[(b, j)][:, P * g : P * (g + 1)],
-                    rhs=w_codes[chunk][:, g, :].bitcast(E2M1X4),
-                    rhs_scale=plane[:, g, N * chunk : N * (chunk + 1)],
-                    start=(g == 0),
-                    stop=(g == PASSES - 1),
+        def quantise_batch(b):
+            for j in range(TILES):
+                pairs = x_rows[(b, j)][:].bitcast(F32)
+                turned = psum.tile([P, PASSES, 2, P], F32, name="xt_%d_%d" % (b, j), tag="bank")
+                for g in range(PASSES):
+                    for u in range(2):
+                        first = K_PASS // 2 * g
+                        nc.tensor.transpose(turned[:, g, u, :], pairs[:, first + u : first + K_PASS // 2 : 2], identity[:])
+                grouped = keep.tile([P, C], BF16, name="xg_%d_%d" % (b, j), align_bytes=MX_ALIGN)
+                dst = grouped[:].bitcast(F32).rearrange("p (g r u) -> p g r u", g=PASSES, u=2)
+                src = turned[:].rearrange("p g u r -> p g r u")
+                if b == 0 and j % 2 == 0:
+                    nc.vector.tensor_copy(out=dst, in_=src)
+                else:
+                    nc.scalar.copy(out=dst, in_=src)
+                words = keep.tile([P, PASSES, P], U32, name="xc_%d_%d" % (b, j), align_bytes=MX_ALIGN)
+                scales = keep.tile([P, PASSES, P], U8, name="xs_%d_%d" % (b, j), align_bytes=MX_ALIGN)
+                nc.vector.quantize_mx(
+                    out=words[:].rearrange("p g r -> p (g r)").bitcast(E5M2X4),
+                    scales=scales[:].rearrange("p g r -> p (g r)"),
+                    in_=grouped[:],
                 )
-            banks[n] = bank
+                x_words[(b, j)] = words
+                x_scales[(b, j)] = scales
 
-        stored = []
+        def project(unit, j0):
+            kind, b, h0 = unit
+            col = FIRST_COL[kind] + D * h0
+            first = col % CHUNK
+            bank = psum.tile([P, BANK_TILES, UNIT_COLS], F32, name="acc_%s_%d_%d_%d" % (unit + (j0,)), tag="bank")
+            for i in range(BANK_TILES):
+                for g in range(PASSES):
+                    nc.tensor.matmul_mx(
+                        out=bank[:, i, :],
+                        lhsT=x_words[(b, j0 + i)][:, g, :].bitcast(E5M2X4),
+                        lhsT_scale=x_scales[(b, j0 + i)][:, g, :],
+                        rhs=w_words[col // CHUNK][:, g, 2 * first : 2 * (first + UNIT_COLS)].bitcast(E2M1X4),
+                        rhs_scale=w_scales[:, g, col : col + UNIT_COLS],
+                        start=(g == 0),
+                        stop=(g == PASSES - 1),
+                    )
+            return bank
 
-        def store(group):
-            kind, b, c = group
-            stored.append(group)
-            dst = outs[kind][b, HEADS * c : HEADS * (c + 1), :, :].rearrange("h (p j) d -> p h (j d)", j=J)
-            nc.sync.dma_start(out=dst, in_=stage[group][:].rearrange("p h j d -> p h (j d)"))
+        def by_head(tiles):
+            return tiles.rearrange("p j (h d) -> p j h d", d=D)
 
-        def add_bias(n):
-            group = groups[n // J]
-            kind, b, c = group
-            j = n % J
-            bias_cols = bias[kind][:, N * c : N * (c + 1)]
-            if kind == "v":
-                nc.vector.tensor_tensor(
-                    stage[group][:, :, j, :],
-                    banks[n][:].rearrange("p (h d) -> p h d", d=D),
-                    bias_cols.rearrange("p (h d) -> p h d", d=D),
-                    op=ALU.add,
-                )
-                if j == J - 1:
-                    store(group)
-            else:
-                if j % 2 == 0:
-                    q_raw[n // 2] = work.tile([P, 2, N], F32, name="q_raw_%d" % n, tag="q_raw", bufs=4)
-                nc.vector.tensor_tensor(q_raw[n // 2][:, j % 2, :], banks[n][:], bias_cols, op=ALU.add)
-
-        def squares(src, dst):
-            junk = work.tile([P, N], F32, name="junk", tag="junk", bufs=3)
-            for h in range(HEADS):
-                nc.scalar.activation(
-                    junk[:, D * h : D * (h + 1)], src[:, D * h : D * (h + 1)], ACT.Square, accum_out=dst[:, h : h + 1]
-                )
-                if h == 1:
-                    flush()
-
-        def k_squares(n):
-            total = keep.tile([P, HEADS], F32, name="k_sum_%d" % n)
-            squares(banks[n][:], total[:])
-
-            def root():
-                r = keep.tile([P, HEADS], F32, name="k_inv_%d" % n)
-                nc.scalar.activation(r[:], total[:], ACT.Abs_reciprocal_sqrt)
-                inv_norm[n] = r
-
-            pending.append(root)
-
-        def k_normalise(n):
-            group = groups[n // J]
-            j = n % J
-            if n not in inv_norm:
-                flush()
-            nc.vector.scalar_tensor_tensor(
-                out=stage[group][:, :, j, :],
-                in0=inv_norm[n][:].unsqueeze(2).to_broadcast([P, HEADS, D]),
-                scalar=MAX_INV_NORM,
-                in1=banks[n][:].rearrange("p (h d) -> p h d", d=D),
-                op0=ALU.min,
-                op1=ALU.mult,
+        def add_bias(unit, bank, out):
+            kind, b, h0 = unit
+            cols = bias[kind][:, D * h0 : D * h0 + UNIT_COLS].rearrange("p (h d) -> p h d", d=D)
+            nc.vector.tensor_tensor(
+                out, by_head(bank[:]), cols.unsqueeze(1).to_broadcast([P, BANK_TILES, UNIT_HEADS, D]), op=ALU.add
             )
-            if j == J - 1:
-                store(group)
 
-        q_done = []
+        def sums_on_scalar(values, sums):
+            squares = work.tile([P, BANK], F32, name="squares", tag="squares")
+            for s in range(BANK_SUMS):
+                cols = slice(D * s, D * (s + 1))
+                nc.scalar.activation(squares[:, cols], values[:, cols], ACT.Square, accum_out=sums[:, s : s + 1])
 
-        def q_squares(n):
-            group = groups[n // J]
-            kind, b, c = group
-            j = n % J
-            pair = n // 2
-            if j % 2 == 0:
-                sums[pair] = keep.tile([P, 2, HEADS], F32, name="q_sum_%d" % n)
-            squares(q_raw[pair][:, j % 2, :], sums[pair][:, j % 2, :])
-            if j % 2 == 0:
-                return
-
-            def normalise():
-                r = keep.tile([P, 2, HEADS], F32, name="q_inv_%d" % n)
-                nc.scalar.activation(r[:], sums[pair][:], ACT.Abs_reciprocal_sqrt)
-                capped = keep.tile([P, 2, HEADS], F32, name="q_cap_%d" % n)
-                nc.gpsimd.tensor_scalar(capped[:], r[:], MAX_INV_NORM, 0.0, op0=ALU.min, op1=ALU.max)
-                factor = keep.tile([P, 2, HEADS], F32, name="q_fac_%d" % n)
-                nc.gpsimd.tensor_tensor(
-                    factor[:],
-                    capped[:],
-                    scale[:, HEADS * c : HEADS * (c + 1)].unsqueeze(1).to_broadcast([P, 2, HEADS]),
-                    op=ALU.mult,
+        def sums_on_vector(values, sums, name):
+            stats = keep.tile([P, BANK_SUMS, 3], F32, name="stats_" + name)
+            for s in range(0, BANK_SUMS, 2):
+                nc.vector.bn_stats(
+                    stats[:, s : s + 2, :].rearrange("p s t -> p (s t)"),
+                    values[:, D * s : D * (s + 2)].rearrange("p (s d) -> p d s", d=D),
                 )
-                nc.gpsimd.tensor_tensor(
-                    stage[group][:, :, j - 1 : j + 1, :].rearrange("p h j d -> p j h d"),
-                    q_raw[pair][:].rearrange("p j (h d) -> p j h d", d=D),
-                    factor[:].unsqueeze(3).to_broadcast([P, 2, HEADS, D]),
-                    op=ALU.mult,
-                )
-                if j == J - 1:
-                    q_done.append(group)
+            nc.scalar.activation(stats[:, :, 1], stats[:, :, 1], ACT.Square, scale=math.sqrt(D))
+            nc.vector.tensor_reduce(sums, stats[:, :, 1:3], axis=mybir.AxisListType.X, op=ALU.add)
 
-            pending.append(normalise)
+        def values_unit(unit, staged, name):
+            for j0 in range(0, TILES, BANK_TILES):
+                add_bias(unit, project(unit, j0), staged[:, j0 : j0 + BANK_TILES, :, :])
 
-        def kind_of(n):
-            return groups[n // J][0] if 0 <= n < n_banks else None
+        def keys_unit(unit, staged, name):
+            for j0 in range(0, TILES, BANK_TILES):
+                bank = project(unit, j0)
+                sums = keep.tile([P, BANK_SUMS], F32, name="sums_%s_%d" % (name, j0))
+                sums_on_scalar(bank[:].rearrange("p j c -> p (j c)"), sums[:])
+                inverse = keep.tile([P, BANK_TILES, UNIT_HEADS], F32, name="inv_%s_%d" % (name, j0))
+                nc.scalar.activation(inverse[:].rearrange("p j h -> p (j h)"), sums[:], ACT.Abs_reciprocal_sqrt)
+                for i in range(BANK_TILES):
+                    nc.vector.scalar_tensor_tensor(
+                        out=staged[:, j0 + i, :, :],
+                        in0=inverse[:, i, :].unsqueeze(2).to_broadcast([P, UNIT_HEADS, D]),
+                        scalar=1.0 / EPS,
+                        in1=by_head(bank[:])[:, i, :, :],
+                        op0=ALU.min,
+                        op1=ALU.mult,
+                    )
 
-        for n in range(n_banks + K_LAG + 1):
-            if n == J:
-                for j in range(J):
-                    transpose_x(1, j)
-                k_squares(n - 1)
-                k_normalise(n - K_LAG)
-                for j in range(J):
-                    copy_x(1, j, j % 2 == 0)
-                    if j == 1:
-                        flush()
-                        k_normalise(n - K_LAG + 1)
-                    if j > 0:
-                        quantize_x(1, j - 1)
-                k_normalise(n - K_LAG + 2)
-                quantize_x(1, J - 1)
-            if n < n_banks:
-                matmul(n)
-            if kind_of(n - 2) == "q":
-                q_squares(n - 2)
-            if kind_of(n - 1) == "k" and n != J:
-                k_squares(n - 1)
-            if kind_of(n - 1) in ("q", "v"):
-                add_bias(n - 1)
-            if kind_of(n - K_LAG) == "k" and not (J <= n < J + K_LAG):
-                k_normalise(n - K_LAG)
-            for group in list(q_done):
-                if ("v",) + group[1:] in stored or group == groups[-3]:
-                    store(group)
-                    q_done.remove(group)
-        assert len(stored) == len(groups) and not pending
+        def queries_unit(unit, staged, name):
+            kind, b, h0 = unit
+            raw = work.tile([P, TILES, UNIT_COLS], F32, name="raw_" + name, tag="raw")
+            sums = keep.tile([P, TILES * UNIT_HEADS], F32, name="sums_" + name)
+            for j0 in range(0, TILES, BANK_TILES):
+                tiles = raw[:, j0 : j0 + BANK_TILES, :]
+                add_bias(unit, project(unit, j0), by_head(tiles))
+                bank_sums = sums[:, UNIT_HEADS * j0 : UNIT_HEADS * j0 + BANK_SUMS]
+                if j0 == 0:
+                    sums_on_vector(tiles.rearrange("p j c -> p (j c)"), bank_sums, name)
+                else:
+                    sums_on_scalar(tiles.rearrange("p j c -> p (j c)"), bank_sums)
+            excess = keep.tile([P, TILES * UNIT_HEADS], F32, name="exc_" + name)
+            nc.scalar.activation(excess[:], sums[:], ACT.Relu, bias=-EPS * EPS)
+            inverse = keep.tile([P, TILES, UNIT_HEADS], F32, name="inv_" + name)
+            nc.scalar.activation(
+                inverse[:].rearrange("p j h -> p (j h)"), excess[:], ACT.Abs_reciprocal_sqrt, bias=EPS * EPS
+            )
+            factor = keep.tile([P, TILES, UNIT_HEADS], F32, name="fac_" + name)
+            scales = head_scale[:, h0 : h0 + UNIT_HEADS].unsqueeze(1).to_broadcast([P, TILES, UNIT_HEADS])
+            nc.gpsimd.tensor_tensor(factor[:], inverse[:], scales, op=ALU.mult)
+            nc.gpsimd.tensor_tensor(
+                staged, by_head(raw[:]), factor[:].unsqueeze(3).to_broadcast([P, TILES, UNIT_HEADS, D]), op=ALU.mult
+            )
+
+        finish = {"q": queries_unit, "k": keys_unit, "v": values_unit}
+        quantise_batch(0)
+        for n, unit in enumerate(units):
+            if n == 2 * LEAD_PAIRS + 1:
+                quantise_batch(1)
+            kind, b, h0 = unit
+            name = "%s_%d_%d" % unit
+            stage = keep.tile([P, UNIT_HEADS, TILES, D], F32, name="stage_" + name, align_bytes=DMA_ALIGN)
+            finish[kind](unit, stage[:].rearrange("p h j d -> p j h d"), name)
+            nc.sync.dma_start(
+                out=outs[kind][b, h0 : h0 + UNIT_HEADS, :, :].rearrange("h (p j) d -> p h (j d)", j=TILES),
+                in_=stage[:].rearrange("p h j d -> p h (j d)"),
+            )

@@ -21,32 +21,34 @@ ACT = mybir.ActivationFunctionType
 P = 128
 K_PASS = 4 * P
 PASSES = C // K_PASS
-TILES = L // P
+TILES = B * L // P
+LOAD_TILES = 2
 BANK = 512
-CHUNK = 512
-UNIT_HEADS = 4
-UNIT_COLS = UNIT_HEADS * D
-UNITS = B * H // UNIT_HEADS
-BANK_TILES = BANK // UNIT_COLS
-BANK_SUMS = BANK_TILES * UNIT_HEADS
+JOB_HEADS = 2
+JOB_COLS = JOB_HEADS * D
+JOB_TILES = BANK // JOB_COLS
+JOB_SUMS = JOB_TILES * JOB_HEADS
 FIRST_COL = {"q": 0, "k": C, "v": 2 * C}
 DMA_ALIGN = 256
 MX_ALIGN = 64
 MAX_LOG_SCALE = math.log(100.0)
 EPS = 1e-12
-LEAD_PAIRS = 3
-EARLY_CHUNKS = 3
+
+ROUND = 3
+Q_SUMS_LAG = 2
+Q_MEAN_LAG = 4
+K_ROOT_LAG = ROUND
+FINISH_LAG = 2 * ROUND
+Q_STORE_LAG = 3 * ROUND
 
 
-def unit_order():
-    order = []
-    for u in range(LEAD_PAIRS):
-        order.extend([("k", u), ("v", u)])
-    others = [(kind, u) for u in range(LEAD_PAIRS, UNITS) for kind in ("v", "k")]
-    for u in range(UNITS):
-        order.extend([("q", u), others[u]])
-    order.extend(others[UNITS:])
-    return order
+def job_order():
+    places = [(h0, j0) for h0 in range(0, H, JOB_HEADS) for j0 in range(0, TILES, JOB_TILES)]
+    jobs = [("q",) + places[0]]
+    for behind, ahead in zip(places, places[1:]):
+        jobs.extend([("k",) + behind, ("q",) + ahead, ("v",) + behind])
+    jobs.extend([("k",) + places[-1], ("v",) + places[-1]])
+    return jobs
 
 
 def tile_selfattention_pa_kernel(
@@ -54,14 +56,12 @@ def tile_selfattention_pa_kernel(
 ):
     nc = tc.nc
     outs = {"q": out_0, "k": out_1, "v": out_2}
-    per_batch = UNITS // B
-    units = [(kind, u // per_batch, UNIT_HEADS * (u % per_batch)) for kind, u in unit_order()]
 
     with ExitStack() as ctx:
         keep = ctx.enter_context(tc.tile_pool(name="keep", bufs=1))
         work = ctx.enter_context(tc.tile_pool(name="work", bufs=4))
         psum = ctx.enter_context(tc.psum_pool(name="psum", bufs=8))
-        ctx.enter_context(tc.manual_schedule(engines={mybir.EngineType.PE}))
+        ctx.enter_context(tc.manual_schedule())
 
         identity = keep.tile([P, P], F32, name="identity")
         make_identity(nc, identity[:])
@@ -80,41 +80,28 @@ def tile_selfattention_pa_kernel(
         nc.scalar.dma_start(out=bias_rows[0:1, C : 2 * C], in_=v_bias.rearrange("(o n) -> o n", o=1))
 
         x_rows = {}
+
+        def load_x(j0):
+            rows = keep.tile([P, LOAD_TILES * C], BF16, name="x_%d" % j0, align_bytes=DMA_ALIGN)
+            src = x.rearrange("b (g j) c -> g b (j c)", j=TILES)[:, :, C * j0 : C * (j0 + LOAD_TILES)]
+            nc.sync.dma_start(out=rows[:], in_=src)
+            for i in range(LOAD_TILES):
+                x_rows[j0 + i] = rows[:, C * i : C * (i + 1)]
+
+        for j0 in range(0, TILES // 2, LOAD_TILES):
+            load_x(j0)
+        for quad in range(4):
+            nc.sync.dma_start(
+                out=w_scales[32 * quad : 32 * quad + 4, :, :].bitcast(I32),
+                in_=W_qkv_scales[:, 4 * quad : 4 * quad + 4, :].rearrange("g r n -> r g n").bitcast(I32),
+            )
+        for j0 in range(TILES // 2, TILES, LOAD_TILES):
+            load_x(j0)
         w_words = {}
-
-        def load_x(b, j):
-            rows = keep.tile([P, C], BF16, name="x_%d_%d" % (b, j), align_bytes=DMA_ALIGN)
-            nc.sync.dma_start(out=rows[:], in_=x[b].rearrange("(p j) c -> p j c", j=TILES)[:, j, :])
-            x_rows[(b, j)] = rows
-
-        def load_w(chunk):
-            words = keep.tile([P, PASSES, 2 * CHUNK], U8, name="w_%d" % chunk, align_bytes=DMA_ALIGN)
-            src = W_qkv_words[:, :, 2 * CHUNK * chunk : 2 * CHUNK * (chunk + 1)].rearrange("g p w -> p g w")
-            nc.sync.dma_start(out=words[:].bitcast(I32), in_=src.bitcast(I32))
-            w_words[chunk] = words
-
-        chunks = []
-        for kind, b, h0 in units:
-            chunk = (FIRST_COL[kind] + D * h0) // CHUNK
-            if chunk not in chunks:
-                chunks.append(chunk)
-        with tc.manual_schedule(engines={mybir.EngineType.SP}):
-            load_x(0, 0)
-            load_x(0, 1)
-            load_w(chunks[0])
-            for quad in range(4):
-                nc.sync.dma_start(
-                    out=w_scales[32 * quad : 32 * quad + 4, :, :].bitcast(I32),
-                    in_=W_qkv_scales[:, 4 * quad : 4 * quad + 4, :].rearrange("g r n -> r g n").bitcast(I32),
-                )
-            load_x(0, 2)
-            load_x(0, 3)
-            for chunk in chunks[1:EARLY_CHUNKS]:
-                load_w(chunk)
-            for j in range(TILES):
-                load_x(1, j)
-            for chunk in chunks[EARLY_CHUNKS:]:
-                load_w(chunk)
+        for kind in ("q", "k", "v"):
+            w_words[kind] = keep.tile([P, PASSES, 2 * C], U8, name="w_%s" % kind, align_bytes=DMA_ALIGN)
+            src = W_qkv_words[:, :, 2 * FIRST_COL[kind] : 2 * (FIRST_COL[kind] + C)].rearrange("g p w -> p g w")
+            nc.sync.dma_start(out=w_words[kind][:].bitcast(I32), in_=src.bitcast(I32))
 
         clamped = keep.tile([P, H], F32, name="clamped")
         nc.vector.tensor_scalar(clamped[:], log_scale[:], MAX_LOG_SCALE, None, op0=ALU.min)
@@ -141,132 +128,181 @@ def tile_selfattention_pa_kernel(
 
         x_words = {}
         x_scales = {}
+        pass_pairs = K_PASS // 2
+        for j in range(TILES):
+            pairs = x_rows[j].bitcast(F32)
+            turned = psum.tile([P, PASSES, 2, P], F32, name="xt_%d" % j, tag="bank")
+            for g in range(PASSES):
+                for u in range(2):
+                    nc.tensor.transpose(
+                        turned[:, g, u, :], pairs[:, pass_pairs * g + u : pass_pairs * (g + 1) : 2], identity[:]
+                    )
+            grouped = keep.tile([P, C], BF16, name="xg_%d" % j, align_bytes=MX_ALIGN)
+            nc.scalar.copy(
+                out=grouped[:].bitcast(F32).rearrange("p (g r u) -> p g r u", g=PASSES, u=2),
+                in_=turned[:].rearrange("p g u r -> p g r u"),
+            )
+            x_words[j] = keep.tile([P, PASSES, P], U32, name="xc_%d" % j, align_bytes=MX_ALIGN)
+            x_scales[j] = keep.tile([P, PASSES, P], U8, name="xs_%d" % j, align_bytes=MX_ALIGN)
+            nc.vector.quantize_mx(
+                out=x_words[j][:].rearrange("p g r -> p (g r)").bitcast(E5M2X4),
+                scales=x_scales[j][:].rearrange("p g r -> p (g r)"),
+                in_=grouped[:],
+            )
 
-        def quantise_batch(b):
-            for j in range(TILES):
-                pairs = x_rows[(b, j)][:].bitcast(F32)
-                turned = psum.tile([P, PASSES, 2, P], F32, name="xt_%d_%d" % (b, j), tag="bank")
-                for g in range(PASSES):
-                    for u in range(2):
-                        first = K_PASS // 2 * g
-                        nc.tensor.transpose(turned[:, g, u, :], pairs[:, first + u : first + K_PASS // 2 : 2], identity[:])
-                grouped = keep.tile([P, C], BF16, name="xg_%d_%d" % (b, j), align_bytes=MX_ALIGN)
-                dst = grouped[:].bitcast(F32).rearrange("p (g r u) -> p g r u", g=PASSES, u=2)
-                src = turned[:].rearrange("p g u r -> p g r u")
-                if b == 0 and j % 2 == 0:
-                    nc.vector.tensor_copy(out=dst, in_=src)
-                else:
-                    nc.scalar.copy(out=dst, in_=src)
-                words = keep.tile([P, PASSES, P], U32, name="xc_%d_%d" % (b, j), align_bytes=MX_ALIGN)
-                scales = keep.tile([P, PASSES, P], U8, name="xs_%d_%d" % (b, j), align_bytes=MX_ALIGN)
-                nc.vector.quantize_mx(
-                    out=words[:].rearrange("p g r -> p (g r)").bitcast(E5M2X4),
-                    scales=scales[:].rearrange("p g r -> p (g r)"),
-                    in_=grouped[:],
-                )
-                x_words[(b, j)] = words
-                x_scales[(b, j)] = scales
+        banks = {}
+        stages = {}
+        k_sums = {}
+        k_inverse = {}
+        q_raw = {}
+        q_sums = {}
+        q_stats = {}
 
-        def project(unit, j0):
-            kind, b, h0 = unit
-            col = FIRST_COL[kind] + D * h0
-            first = col % CHUNK
-            bank = psum.tile([P, BANK_TILES, UNIT_COLS], F32, name="acc_%s_%d_%d_%d" % (unit + (j0,)), tag="bank")
-            for i in range(BANK_TILES):
+        def project(job):
+            kind, h0, j0 = job
+            col = D * h0
+            banks[job] = psum.tile([P, JOB_TILES, JOB_COLS], F32, name="acc_%s_%d_%d" % job, tag="bank")
+            for i in range(JOB_TILES):
                 for g in range(PASSES):
                     nc.tensor.matmul_mx(
-                        out=bank[:, i, :],
-                        lhsT=x_words[(b, j0 + i)][:, g, :].bitcast(E5M2X4),
-                        lhsT_scale=x_scales[(b, j0 + i)][:, g, :],
-                        rhs=w_words[col // CHUNK][:, g, 2 * first : 2 * (first + UNIT_COLS)].bitcast(E2M1X4),
-                        rhs_scale=w_scales[:, g, col : col + UNIT_COLS],
+                        out=banks[job][:, i, :],
+                        lhsT=x_words[j0 + i][:, g, :].bitcast(E5M2X4),
+                        lhsT_scale=x_scales[j0 + i][:, g, :],
+                        rhs=w_words[kind][:, g, 2 * col : 2 * (col + JOB_COLS)].bitcast(E2M1X4),
+                        rhs_scale=w_scales[:, g, FIRST_COL[kind] + col : FIRST_COL[kind] + col + JOB_COLS],
                         start=(g == 0),
                         stop=(g == PASSES - 1),
                     )
-            return bank
+            if j0 == 0:
+                stages[(kind, h0)] = keep.tile(
+                    [P, JOB_HEADS, TILES, D], F32, name="stage_%s_%d" % (kind, h0), align_bytes=DMA_ALIGN
+                )
 
         def by_head(tiles):
             return tiles.rearrange("p j (h d) -> p j h d", d=D)
 
-        def add_bias(unit, bank, out):
-            kind, b, h0 = unit
-            cols = bias[kind][:, D * h0 : D * h0 + UNIT_COLS].rearrange("p (h d) -> p h d", d=D)
+        def staged(kind, h0):
+            return stages[(kind, h0)][:].rearrange("p h j d -> p j h d")
+
+        def is_second(job):
+            return job[2] + JOB_TILES == TILES
+
+        def store(job):
+            kind, h0, j0 = job
+            if is_second(job):
+                for h in range(JOB_HEADS):
+                    nc.sync.dma_start(
+                        out=outs[kind].rearrange("b h (g j) d -> g b h (j d)", j=TILES)[:, :, h0 + h, :],
+                        in_=stages[(kind, h0)][:, h, :, :].rearrange("p j d -> p (j d)"),
+                    )
+
+        def add_bias(job, out):
+            kind, h0, j0 = job
+            cols = bias[kind][:, D * h0 : D * h0 + JOB_COLS].rearrange("p (h d) -> p h d", d=D)
             nc.vector.tensor_tensor(
-                out, by_head(bank[:]), cols.unsqueeze(1).to_broadcast([P, BANK_TILES, UNIT_HEADS, D]), op=ALU.add
+                out, by_head(banks[job][:]), cols.unsqueeze(1).to_broadcast([P, JOB_TILES, JOB_HEADS, D]), op=ALU.add
             )
 
         def sums_on_scalar(values, sums):
             squares = work.tile([P, BANK], F32, name="squares", tag="squares")
-            for s in range(BANK_SUMS):
+            for s in range(JOB_SUMS):
                 cols = slice(D * s, D * (s + 1))
                 nc.scalar.activation(squares[:, cols], values[:, cols], ACT.Square, accum_out=sums[:, s : s + 1])
 
-        def sums_on_vector(values, sums, name):
-            stats = keep.tile([P, BANK_SUMS, 3], F32, name="stats_" + name)
-            for s in range(0, BANK_SUMS, 2):
+        def v_finish(job):
+            kind, h0, j0 = job
+            add_bias(job, staged(kind, h0)[:, j0 : j0 + JOB_TILES, :, :])
+            store(job)
+
+        def k_squares(job):
+            k_sums[job] = keep.tile([P, JOB_SUMS], F32, name="sums_%s_%d_%d" % job)
+            sums_on_scalar(banks[job][:].rearrange("p j c -> p (j c)"), k_sums[job][:])
+
+        def k_root(job):
+            k_inverse[job] = keep.tile([P, JOB_TILES, JOB_HEADS], F32, name="inv_%s_%d_%d" % job)
+            nc.scalar.activation(k_inverse[job][:].rearrange("p j h -> p (j h)"), k_sums[job][:], ACT.Abs_reciprocal_sqrt)
+
+        def k_finish(job):
+            kind, h0, j0 = job
+            for h in range(JOB_HEADS):
+                nc.vector.scalar_tensor_tensor(
+                    out=staged(kind, h0)[:, j0 : j0 + JOB_TILES, h, :],
+                    in0=k_inverse[job][:, :, h : h + 1].to_broadcast([P, JOB_TILES, D]),
+                    scalar=1.0 / EPS,
+                    in1=by_head(banks[job][:])[:, :, h, :],
+                    op0=ALU.min,
+                    op1=ALU.mult,
+                )
+            store(job)
+
+        def q_add(job):
+            kind, h0, j0 = job
+            if j0 == 0:
+                q_raw[h0] = work.tile([P, TILES, JOB_COLS], F32, name="raw_%d" % h0, tag="raw")
+                q_sums[h0] = keep.tile([P, TILES * JOB_HEADS], F32, name="sums_q_%d" % h0)
+            add_bias(job, by_head(q_raw[h0][:, j0 : j0 + JOB_TILES, :]))
+
+        def q_squares(job):
+            kind, h0, j0 = job
+            values = q_raw[h0][:, j0 : j0 + JOB_TILES, :].rearrange("p j c -> p (j c)")
+            if is_second(job):
+                sums_on_scalar(values, q_sums[h0][:, JOB_SUMS : 2 * JOB_SUMS])
+                return
+            q_stats[h0] = keep.tile([P, JOB_SUMS, 3], F32, name="stats_q_%d" % h0)
+            for s in range(0, JOB_SUMS, 2):
                 nc.vector.bn_stats(
-                    stats[:, s : s + 2, :].rearrange("p s t -> p (s t)"),
+                    q_stats[h0][:, s : s + 2, :].rearrange("p s t -> p (s t)"),
                     values[:, D * s : D * (s + 2)].rearrange("p (s d) -> p d s", d=D),
                 )
-            nc.scalar.activation(stats[:, :, 1], stats[:, :, 1], ACT.Square, scale=math.sqrt(D))
-            nc.vector.tensor_reduce(sums, stats[:, :, 1:3], axis=mybir.AxisListType.X, op=ALU.add)
 
-        def values_unit(unit, staged, name):
-            for j0 in range(0, TILES, BANK_TILES):
-                add_bias(unit, project(unit, j0), staged[:, j0 : j0 + BANK_TILES, :, :])
+        def q_mean(job):
+            if not is_second(job):
+                means = q_stats[job[1]][:, :, 1]
+                nc.scalar.activation(means, means, ACT.Square, scale=math.sqrt(D))
 
-        def keys_unit(unit, staged, name):
-            for j0 in range(0, TILES, BANK_TILES):
-                bank = project(unit, j0)
-                sums = keep.tile([P, BANK_SUMS], F32, name="sums_%s_%d" % (name, j0))
-                sums_on_scalar(bank[:].rearrange("p j c -> p (j c)"), sums[:])
-                inverse = keep.tile([P, BANK_TILES, UNIT_HEADS], F32, name="inv_%s_%d" % (name, j0))
-                nc.scalar.activation(inverse[:].rearrange("p j h -> p (j h)"), sums[:], ACT.Abs_reciprocal_sqrt)
-                for i in range(BANK_TILES):
-                    nc.vector.scalar_tensor_tensor(
-                        out=staged[:, j0 + i, :, :],
-                        in0=inverse[:, i, :].unsqueeze(2).to_broadcast([P, UNIT_HEADS, D]),
-                        scalar=1.0 / EPS,
-                        in1=by_head(bank[:])[:, i, :, :],
-                        op0=ALU.min,
-                        op1=ALU.mult,
-                    )
+        def q_total(job):
+            if not is_second(job):
+                h0 = job[1]
+                nc.vector.tensor_reduce(
+                    q_sums[h0][:, 0:JOB_SUMS], q_stats[h0][:, :, 1:3], axis=mybir.AxisListType.X, op=ALU.add
+                )
 
-        def queries_unit(unit, staged, name):
-            kind, b, h0 = unit
-            raw = work.tile([P, TILES, UNIT_COLS], F32, name="raw_" + name, tag="raw")
-            sums = keep.tile([P, TILES * UNIT_HEADS], F32, name="sums_" + name)
-            for j0 in range(0, TILES, BANK_TILES):
-                tiles = raw[:, j0 : j0 + BANK_TILES, :]
-                add_bias(unit, project(unit, j0), by_head(tiles))
-                bank_sums = sums[:, UNIT_HEADS * j0 : UNIT_HEADS * j0 + BANK_SUMS]
-                if j0 == 0:
-                    sums_on_vector(tiles.rearrange("p j c -> p (j c)"), bank_sums, name)
-                else:
-                    sums_on_scalar(tiles.rearrange("p j c -> p (j c)"), bank_sums)
-            excess = keep.tile([P, TILES * UNIT_HEADS], F32, name="exc_" + name)
-            nc.scalar.activation(excess[:], sums[:], ACT.Relu, bias=-EPS * EPS)
-            inverse = keep.tile([P, TILES, UNIT_HEADS], F32, name="inv_" + name)
+        def q_finish(job):
+            kind, h0, j0 = job
+            if not is_second(job):
+                return
+            excess = keep.tile([P, TILES * JOB_HEADS], F32, name="exc_%d" % h0)
+            nc.scalar.activation(excess[:], q_sums[h0][:], ACT.Relu, bias=-EPS * EPS)
+            inverse = keep.tile([P, TILES, JOB_HEADS], F32, name="inv_q_%d" % h0)
             nc.scalar.activation(
                 inverse[:].rearrange("p j h -> p (j h)"), excess[:], ACT.Abs_reciprocal_sqrt, bias=EPS * EPS
             )
-            factor = keep.tile([P, TILES, UNIT_HEADS], F32, name="fac_" + name)
-            scales = head_scale[:, h0 : h0 + UNIT_HEADS].unsqueeze(1).to_broadcast([P, TILES, UNIT_HEADS])
+            factor = keep.tile([P, TILES, JOB_HEADS], F32, name="fac_%d" % h0)
+            scales = head_scale[:, h0 : h0 + JOB_HEADS].unsqueeze(1).to_broadcast([P, TILES, JOB_HEADS])
             nc.gpsimd.tensor_tensor(factor[:], inverse[:], scales, op=ALU.mult)
             nc.gpsimd.tensor_tensor(
-                staged, by_head(raw[:]), factor[:].unsqueeze(3).to_broadcast([P, TILES, UNIT_HEADS, D]), op=ALU.mult
+                staged(kind, h0),
+                by_head(q_raw[h0][:]),
+                factor[:].unsqueeze(3).to_broadcast([P, TILES, JOB_HEADS, D]),
+                op=ALU.mult,
             )
 
-        finish = {"q": queries_unit, "k": keys_unit, "v": values_unit}
-        quantise_batch(0)
-        for n, unit in enumerate(units):
-            if n == 2 * LEAD_PAIRS + 1:
-                quantise_batch(1)
-            kind, b, h0 = unit
-            name = "%s_%d_%d" % unit
-            stage = keep.tile([P, UNIT_HEADS, TILES, D], F32, name="stage_" + name, align_bytes=DMA_ALIGN)
-            finish[kind](unit, stage[:].rearrange("p h j d -> p j h d"), name)
-            nc.sync.dma_start(
-                out=outs[kind][b, h0 : h0 + UNIT_HEADS, :, :].rearrange("h (p j) d -> p h (j d)", j=TILES),
-                in_=stage[:].rearrange("p h j d -> p h (j d)"),
-            )
+        steps = [
+            ("q", Q_MEAN_LAG, q_mean),
+            ("k", K_ROOT_LAG, k_root),
+            ("q", FINISH_LAG, q_finish),
+            ("k", 1, k_squares),
+            ("q", FINISH_LAG, q_total),
+            ("k", FINISH_LAG, k_finish),
+            ("q", 1, q_add),
+            ("v", 1, v_finish),
+            ("q", Q_SUMS_LAG, q_squares),
+            ("q", Q_STORE_LAG, store),
+        ]
+        jobs = job_order()
+        for n in range(len(jobs) + Q_STORE_LAG):
+            if n < len(jobs):
+                project(jobs[n])
+            for kind, lag, step in steps:
+                if 0 <= n - lag < len(jobs) and jobs[n - lag][0] == kind:
+                    step(jobs[n - lag])

import math
from contextlib import ExitStack

import concourse.mybir as mybir
from concourse.masks import make_identity

B, L, C, H = 2, 512, 1024, 16
D = C // H
FLOPS = 2 * B * L * C * 3 * C

F32 = mybir.dt.float32
BF16 = mybir.dt.bfloat16
I32 = mybir.dt.int32
U32 = mybir.dt.uint32
U8 = mybir.dt.uint8
E5M2X4 = mybir.dt.float8_e5m2_x4
E2M1X4 = mybir.dt.float4_e2m1fn_x4
ALU = mybir.AluOpType
ACT = mybir.ActivationFunctionType

P = 128
K_PASS = 4 * P
PASSES = C // K_PASS
TILES = B * L // P
LOAD_TILES = 2
BANK = 512
JOB_HEADS = 2
JOB_COLS = JOB_HEADS * D
JOB_TILES = BANK // JOB_COLS
JOB_SUMS = JOB_TILES * JOB_HEADS
FIRST_COL = {"q": 0, "k": C, "v": 2 * C}
DMA_ALIGN = 256
MX_ALIGN = 64
MAX_LOG_SCALE = math.log(100.0)
EPS = 1e-12

ROUND = 3
Q_SUMS_LAG = 2
Q_MEAN_LAG = 4
K_ROOT_LAG = ROUND
FINISH_LAG = 2 * ROUND
Q_STORE_LAG = 3 * ROUND


def job_order():
    places = [(h0, j0) for h0 in range(0, H, JOB_HEADS) for j0 in range(0, TILES, JOB_TILES)]
    jobs = [("q",) + places[0]]
    for behind, ahead in zip(places, places[1:]):
        jobs.extend([("k",) + behind, ("q",) + ahead, ("v",) + behind])
    jobs.extend([("k",) + places[-1], ("v",) + places[-1]])
    return jobs


def tile_selfattention_pa_kernel(
    tc, x, W_qkv_words, W_qkv_scales, q_bias, v_bias, log_scale_mul, out_0, out_1, out_2
):
    nc = tc.nc
    outs = {"q": out_0, "k": out_1, "v": out_2}

    with ExitStack() as ctx:
        keep = ctx.enter_context(tc.tile_pool(name="keep", bufs=1))
        work = ctx.enter_context(tc.tile_pool(name="work", bufs=4))
        psum = ctx.enter_context(tc.psum_pool(name="psum", bufs=8))
        ctx.enter_context(tc.manual_schedule())

        identity = keep.tile([P, P], F32, name="identity")
        make_identity(nc, identity[:])
        bias_rows = keep.tile([P, 2 * C], BF16, name="bias_rows")
        nc.vector.memset(bias_rows[:].bitcast(I32), 0)
        w_scales = keep.tile([P, PASSES, 3 * C], U8, name="w_scales", align_bytes=DMA_ALIGN)
        nc.vector.memset(w_scales[:].bitcast(I32), 0)
        ones = keep.tile([P, P], BF16, name="ones")
        nc.gpsimd.memset(ones[:], 1.0)

        log_scale = keep.tile([P, H], BF16, name="log_scale")
        nc.scalar.dma_start(
            out=log_scale[:], in_=log_scale_mul.rearrange("a h b c -> (a h b c)").partition_broadcast(P)
        )
        nc.scalar.dma_start(out=bias_rows[0:1, 0:C], in_=q_bias.rearrange("(o n) -> o n", o=1))
        nc.scalar.dma_start(out=bias_rows[0:1, C : 2 * C], in_=v_bias.rearrange("(o n) -> o n", o=1))

        x_rows = {}

        def load_x(j0):
            rows = keep.tile([P, LOAD_TILES * C], BF16, name="x_%d" % j0, align_bytes=DMA_ALIGN)
            src = x.rearrange("b (g j) c -> g b (j c)", j=TILES)[:, :, C * j0 : C * (j0 + LOAD_TILES)]
            nc.sync.dma_start(out=rows[:], in_=src)
            for i in range(LOAD_TILES):
                x_rows[j0 + i] = rows[:, C * i : C * (i + 1)]

        for j0 in range(0, TILES // 2, LOAD_TILES):
            load_x(j0)
        for quad in range(4):
            nc.sync.dma_start(
                out=w_scales[32 * quad : 32 * quad + 4, :, :].bitcast(I32),
                in_=W_qkv_scales[:, 4 * quad : 4 * quad + 4, :].rearrange("g r n -> r g n").bitcast(I32),
            )
        for j0 in range(TILES // 2, TILES, LOAD_TILES):
            load_x(j0)
        w_words = {}
        for kind in ("q", "k", "v"):
            w_words[kind] = keep.tile([P, PASSES, 2 * C], U8, name="w_%s" % kind, align_bytes=DMA_ALIGN)
            src = W_qkv_words[:, :, 2 * FIRST_COL[kind] : 2 * (FIRST_COL[kind] + C)].rearrange("g p w -> p g w")
            nc.sync.dma_start(out=w_words[kind][:].bitcast(I32), in_=src.bitcast(I32))

        clamped = keep.tile([P, H], F32, name="clamped")
        nc.vector.tensor_scalar(clamped[:], log_scale[:], MAX_LOG_SCALE, None, op0=ALU.min)
        inverse_scale = keep.tile([P, H], F32, name="inverse_scale")
        nc.scalar.activation(inverse_scale[:], clamped[:], ACT.Exp, scale=-1.0)
        root_scale = keep.tile([P, H], F32, name="root_scale")
        nc.scalar.activation(root_scale[:], inverse_scale[:], ACT.Abs_reciprocal_sqrt)
        head_scale = keep.tile([P, H], F32, name="head_scale")
        nc.gpsimd.tensor_tensor(head_scale[:], root_scale[:], root_scale[:], op=ALU.mult)

        bias = {}
        for i, kind in enumerate(("q", "v")):
            spread = psum.tile([P, C], BF16, name="bias_bank", tag="bank")
            for col in range(0, C, BANK):
                nc.tensor.matmul(
                    spread[:, col : col + BANK],
                    lhsT=ones[:],
                    rhs=bias_rows[:, C * i + col : C * i + col + BANK],
                    start=True,
                    stop=True,
                )
            bias[kind] = keep.tile([P, C], BF16, name="bias_%s" % kind)
            nc.vector.tensor_copy(out=bias[kind][:], in_=spread[:])

        x_words = {}
        x_scales = {}
        pass_pairs = K_PASS // 2
        for j in range(TILES):
            pairs = x_rows[j].bitcast(F32)
            turned = psum.tile([P, PASSES, 2, P], F32, name="xt_%d" % j, tag="bank")
            for g in range(PASSES):
                for u in range(2):
                    nc.tensor.transpose(
                        turned[:, g, u, :], pairs[:, pass_pairs * g + u : pass_pairs * (g + 1) : 2], identity[:]
                    )
            grouped = keep.tile([P, C], BF16, name="xg_%d" % j, align_bytes=MX_ALIGN)
            nc.scalar.copy(
                out=grouped[:].bitcast(F32).rearrange("p (g r u) -> p g r u", g=PASSES, u=2),
                in_=turned[:].rearrange("p g u r -> p g r u"),
            )
            x_words[j] = keep.tile([P, PASSES, P], U32, name="xc_%d" % j, align_bytes=MX_ALIGN)
            x_scales[j] = keep.tile([P, PASSES, P], U8, name="xs_%d" % j, align_bytes=MX_ALIGN)
            nc.vector.quantize_mx(
                out=x_words[j][:].rearrange("p g r -> p (g r)").bitcast(E5M2X4),
                scales=x_scales[j][:].rearrange("p g r -> p (g r)"),
                in_=grouped[:],
            )

        banks = {}
        stages = {}
        k_sums = {}
        k_inverse = {}
        q_raw = {}
        q_sums = {}
        q_stats = {}

        def project(job):
            kind, h0, j0 = job
            col = D * h0
            banks[job] = psum.tile([P, JOB_TILES, JOB_COLS], F32, name="acc_%s_%d_%d" % job, tag="bank")
            for i in range(JOB_TILES):
                for g in range(PASSES):
                    nc.tensor.matmul_mx(
                        out=banks[job][:, i, :],
                        lhsT=x_words[j0 + i][:, g, :].bitcast(E5M2X4),
                        lhsT_scale=x_scales[j0 + i][:, g, :],
                        rhs=w_words[kind][:, g, 2 * col : 2 * (col + JOB_COLS)].bitcast(E2M1X4),
                        rhs_scale=w_scales[:, g, FIRST_COL[kind] + col : FIRST_COL[kind] + col + JOB_COLS],
                        start=(g == 0),
                        stop=(g == PASSES - 1),
                    )
            if j0 == 0:
                stages[(kind, h0)] = keep.tile(
                    [P, JOB_HEADS, TILES, D], F32, name="stage_%s_%d" % (kind, h0), align_bytes=DMA_ALIGN
                )

        def by_head(tiles):
            return tiles.rearrange("p j (h d) -> p j h d", d=D)

        def staged(kind, h0):
            return stages[(kind, h0)][:].rearrange("p h j d -> p j h d")

        def is_second(job):
            return job[2] + JOB_TILES == TILES

        def store(job):
            kind, h0, j0 = job
            if is_second(job):
                for h in range(JOB_HEADS):
                    nc.sync.dma_start(
                        out=outs[kind].rearrange("b h (g j) d -> g b h (j d)", j=TILES)[:, :, h0 + h, :],
                        in_=stages[(kind, h0)][:, h, :, :].rearrange("p j d -> p (j d)"),
                    )

        def add_bias(job, out):
            kind, h0, j0 = job
            cols = bias[kind][:, D * h0 : D * h0 + JOB_COLS].rearrange("p (h d) -> p h d", d=D)
            nc.vector.tensor_tensor(
                out, by_head(banks[job][:]), cols.unsqueeze(1).to_broadcast([P, JOB_TILES, JOB_HEADS, D]), op=ALU.add
            )

        def sums_on_scalar(values, sums):
            squares = work.tile([P, BANK], F32, name="squares", tag="squares")
            for s in range(JOB_SUMS):
                cols = slice(D * s, D * (s + 1))
                nc.scalar.activation(squares[:, cols], values[:, cols], ACT.Square, accum_out=sums[:, s : s + 1])

        def v_finish(job):
            kind, h0, j0 = job
            add_bias(job, staged(kind, h0)[:, j0 : j0 + JOB_TILES, :, :])
            store(job)

        def k_squares(job):
            k_sums[job] = keep.tile([P, JOB_SUMS], F32, name="sums_%s_%d_%d" % job)
            sums_on_scalar(banks[job][:].rearrange("p j c -> p (j c)"), k_sums[job][:])

        def k_root(job):
            k_inverse[job] = keep.tile([P, JOB_TILES, JOB_HEADS], F32, name="inv_%s_%d_%d" % job)
            nc.scalar.activation(k_inverse[job][:].rearrange("p j h -> p (j h)"), k_sums[job][:], ACT.Abs_reciprocal_sqrt)

        def k_finish(job):
            kind, h0, j0 = job
            for h in range(JOB_HEADS):
                nc.vector.scalar_tensor_tensor(
                    out=staged(kind, h0)[:, j0 : j0 + JOB_TILES, h, :],
                    in0=k_inverse[job][:, :, h : h + 1].to_broadcast([P, JOB_TILES, D]),
                    scalar=1.0 / EPS,
                    in1=by_head(banks[job][:])[:, :, h, :],
                    op0=ALU.min,
                    op1=ALU.mult,
                )
            store(job)

        def q_add(job):
            kind, h0, j0 = job
            if j0 == 0:
                q_raw[h0] = work.tile([P, TILES, JOB_COLS], F32, name="raw_%d" % h0, tag="raw")
                q_sums[h0] = keep.tile([P, TILES * JOB_HEADS], F32, name="sums_q_%d" % h0)
            add_bias(job, by_head(q_raw[h0][:, j0 : j0 + JOB_TILES, :]))

        def q_squares(job):
            kind, h0, j0 = job
            values = q_raw[h0][:, j0 : j0 + JOB_TILES, :].rearrange("p j c -> p (j c)")
            if is_second(job):
                sums_on_scalar(values, q_sums[h0][:, JOB_SUMS : 2 * JOB_SUMS])
                return
            q_stats[h0] = keep.tile([P, JOB_SUMS, 3], F32, name="stats_q_%d" % h0)
            for s in range(0, JOB_SUMS, 2):
                nc.vector.bn_stats(
                    q_stats[h0][:, s : s + 2, :].rearrange("p s t -> p (s t)"),
                    values[:, D * s : D * (s + 2)].rearrange("p (s d) -> p d s", d=D),
                )

        def q_mean(job):
            if not is_second(job):
                means = q_stats[job[1]][:, :, 1]
                nc.scalar.activation(means, means, ACT.Square, scale=math.sqrt(D))

        def q_total(job):
            if not is_second(job):
                h0 = job[1]
                nc.vector.tensor_reduce(
                    q_sums[h0][:, 0:JOB_SUMS], q_stats[h0][:, :, 1:3], axis=mybir.AxisListType.X, op=ALU.add
                )

        def q_finish(job):
            kind, h0, j0 = job
            if not is_second(job):
                return
            excess = keep.tile([P, TILES * JOB_HEADS], F32, name="exc_%d" % h0)
            nc.scalar.activation(excess[:], q_sums[h0][:], ACT.Relu, bias=-EPS * EPS)
            inverse = keep.tile([P, TILES, JOB_HEADS], F32, name="inv_q_%d" % h0)
            nc.scalar.activation(
                inverse[:].rearrange("p j h -> p (j h)"), excess[:], ACT.Abs_reciprocal_sqrt, bias=EPS * EPS
            )
            factor = keep.tile([P, TILES, JOB_HEADS], F32, name="fac_%d" % h0)
            scales = head_scale[:, h0 : h0 + JOB_HEADS].unsqueeze(1).to_broadcast([P, TILES, JOB_HEADS])
            nc.gpsimd.tensor_tensor(factor[:], inverse[:], scales, op=ALU.mult)
            nc.gpsimd.tensor_tensor(
                staged(kind, h0),
                by_head(q_raw[h0][:]),
                factor[:].unsqueeze(3).to_broadcast([P, TILES, JOB_HEADS, D]),
                op=ALU.mult,
            )

        steps = [
            ("q", Q_MEAN_LAG, q_mean),
            ("k", K_ROOT_LAG, k_root),
            ("q", FINISH_LAG, q_finish),
            ("k", 1, k_squares),
            ("q", FINISH_LAG, q_total),
            ("k", FINISH_LAG, k_finish),
            ("q", 1, q_add),
            ("v", 1, v_finish),
            ("q", Q_SUMS_LAG, q_squares),
            ("q", Q_STORE_LAG, store),
        ]
        jobs = job_order()
        for n in range(len(jobs) + Q_STORE_LAG):
            if n < len(jobs):
                project(jobs[n])
            for kind, lag, step in steps:
                if 0 <= n - lag < len(jobs) and jobs[n - lag][0] == kind:
                    step(jobs[n - lag])
